import numpy as np
import ml_dtypes


def mxq(x, axis, fmt="e4m3"):
    dtype, down = {"e4m3": (ml_dtypes.float8_e4m3fn, 7), "e5m2": (ml_dtypes.float8_e5m2, 14)}[fmt]
    v = np.moveaxis(np.asarray(x, np.float32).astype(ml_dtypes.bfloat16).astype(np.float64), axis, -1)
    blocks = v.reshape(v.shape[:-1] + (-1, 32))
    amax = np.abs(blocks).max(-1, keepdims=True)
    byte = np.maximum(np.where(amax > 0, np.frexp(amax)[1] - 1 + 127, 0) - down, 1)
    scale = np.exp2(byte - 127.0)
    codes = (blocks / scale).astype(np.float32).astype(dtype).astype(np.float64)
    return np.moveaxis((codes * scale).reshape(v.shape), -1, axis)


WIDE = False


def mx_kscale(k):
    if not WIDE:
        return np.ones(k)
    levels = np.array([10, -10, 5, -5, 0])
    a = np.random.permutation(np.resize(levels, k // 512 * 4)).reshape(k // 512, 4)
    idx = np.arange(k)
    return np.exp2(a[idx // 512, idx % 128 // 32])


BF16 = ml_dtypes.bfloat16


def bf(x):
    return np.asarray(x, np.float32).astype(BF16)


def f64(x):
    return np.asarray(x).astype(np.float64)


E2M1 = np.array([0.0, 0.5, 1.0, 1.5, 2.0, 3.0, 4.0, 6.0, -0.0, -0.5, -1.0, -1.5, -2.0, -3.0, -4.0, -6.0])


def pack_weight(w, fmt):
    k, n = w.shape
    w = f64(bf(w)).reshape(k // 32, 32, n)
    amax = np.abs(w).max(1)
    if fmt == "e4m3":
        byte = np.frexp(amax)[1] - 1 + 127 - 7
    else:
        mant, ex = np.frexp(amax / 6.0)
        byte = np.where(mant > 0.5, ex, ex - 1) + 127
    byte = np.clip(np.where(amax > 0, byte, 1), 1, 254)
    scaled = (w * np.exp2(127.0 - byte)[:, None, :]).reshape(k, n).astype(np.float32)
    by_word = np.ascontiguousarray(scaled.reshape(k // 512, 128, 4, n).transpose(0, 1, 3, 2))
    if fmt == "e4m3":
        words = by_word.astype(ml_dtypes.float8_e4m3fn).view(np.uint8)
    else:
        c = by_word.astype(ml_dtypes.float4_e2m1fn).view(np.uint8) & 0xF
        words = c[..., 0::2] | (c[..., 1::2] << 4)
    return np.ascontiguousarray(words), np.ascontiguousarray(byte.astype(np.uint8).reshape(k // 512, 16, n))


def unpack_weight(words, scales, fmt):
    g, p, n, _ = words.shape
    if fmt == "e4m3":
        vals = np.ascontiguousarray(words).view(ml_dtypes.float8_e4m3fn).astype(np.float64)
    else:
        nib = np.empty((g, p, n, 4), np.uint8)
        nib[..., 0::2] = words & 0xF
        nib[..., 1::2] = words >> 4
        vals = E2M1[nib]
    vals = vals * np.repeat(np.exp2(scales.astype(np.float64) - 127.0), 8, axis=1)[..., None]
    return vals.transpose(0, 1, 3, 2).reshape(g * 512, n)


B, L0, L1, L2, L3 = 128, 2048, 2048, 4096, 2048
NA = 5
FMT = "e4m3"


def _act(x, a):
    return a[:, 0] * np.tanh(x) * np.sin(a[:, 1] * x + a[:, 2]) + a[:, 3] * x + a[:, 4]


def _gain(t):
    one = np.ones_like(t)
    return np.stack([t, one, one, t, t], axis=1)


def setup_inputs():
    t, u = mx_kscale(L1), mx_kscale(L2)
    data = bf(np.random.standard_normal((B, L0)))
    W1 = bf(np.random.standard_normal((L0, L1)) * 1.0 / np.sqrt(L0))
    b1 = bf(np.random.standard_normal(L1) * 0.1)
    a1 = bf(np.random.random((L1, NA)) * _gain(t))
    W2_words, W2_scales = pack_weight(np.random.standard_normal((L1, L2)) * 1.2 / np.sqrt(L1) / t[:, None], FMT)
    b2 = bf(np.random.standard_normal(L2) * 0.1)
    a2 = bf(np.random.random((L2, NA)) * _gain(u))
    W3_words, W3_scales = pack_weight(np.random.standard_normal((L2, L3)) * 2.0 / np.sqrt(L2) / u[:, None], FMT)
    b3 = bf(np.random.standard_normal(L3) * 0.1)
    a3 = bf(np.random.random((L3, NA)))
    return {"data": data,
            "W1": W1,
            "b1": b1,
            "a1": a1,
            "W2_words": W2_words,
            "W2_scales": W2_scales,
            "b2": b2,
            "a2": a2,
            "W3_words": W3_words,
            "W3_scales": W3_scales,
            "b3": b3,
            "a3": a3}


def reference(data, W1, b1, a1, W2_words, W2_scales, b2, a2, W3_words, W3_scales, b3, a3):
    h = _act(f64(data) @ f64(W1) + f64(b1), f64(a1))
    h = _act((mxq(h, 1, "e4m3") @ unpack_weight(W2_words, W2_scales, FMT)) + f64(b2), f64(a2))
    h = _act((mxq(h, 1, "e4m3") @ unpack_weight(W3_words, W3_scales, FMT)) + f64(b3), f64(a3))
    e = np.exp(h - h.max(axis=1, keepdims=True))
    return e / e.sum(axis=1, keepdims=True)

@@ -1,0 +1,259 @@
+import math
+from contextlib import ExitStack
+
+import concourse.mybir as mybir
+from concourse.masks import make_identity
+
+F32 = mybir.dt.float32
+BF16 = mybir.dt.bfloat16
+I32 = mybir.dt.int32
+U32 = mybir.dt.uint32
+U8 = mybir.dt.uint8
+FP8X4 = mybir.dt.float8_e4m3fn_x4
+AF = mybir.ActivationFunctionType
+ALU = mybir.AluOpType
+AX = mybir.AxisListType
+
+P = 128
+FLOPS = 2 * 128 * (2048 * 2048 + 2048 * 4096 + 4096 * 2048)
+TWO_PI = 2.0 * math.pi
+INV_TWO_PI = 1.0 / TWO_PI
+
+
+def derive(nc, a, bb, d):
+    nc.vector.tensor_scalar(out=d[0], in0=a[1], scalar1=INV_TWO_PI, scalar2=None, op0=ALU.mult)
+    nc.vector.tensor_tensor(out=d[1], in0=a[1], in1=bb, op=ALU.mult)
+    nc.vector.tensor_tensor(out=d[1], in0=d[1], in1=a[2], op=ALU.add)
+    nc.vector.tensor_scalar(out=d[2], in0=d[1], scalar1=INV_TWO_PI, scalar2=None, op0=ALU.mult)
+    nc.vector.tensor_tensor(out=d[3], in0=a[3], in1=bb, op=ALU.mult)
+    nc.vector.tensor_tensor(out=d[3], in0=d[3], in1=a[4], op=ALU.add)
+
+
+def node_act(nc, work, xc, prm, out_ap, permute, label):
+    kk = work.tile([P, 4, P], I32, name="kk_" + label, tag="kk")
+    tt = work.tile([P, 4, P], F32, name="tt_" + label, tag="tt")
+    ww = work.tile([P, 4, P], F32, name="ww_" + label, tag="ww")
+    ll = work.tile([P, 4, P], F32, name="ll_" + label, tag="ll")
+    for t in range(4):
+        nc.vector.tensor_scalar(out=kk[:, t, :], in0=xc[:, t, :], scalar1=prm[t]["a1p"],
+                                scalar2=prm[t]["c2p"], op0=ALU.mult, op1=ALU.add)
+    for t in range(4):
+        nc.scalar.activation(out=tt[:, t, :], in_=xc[:, t, :], func=AF.Tanh, bias=prm[t]["b"], scale=1.0)
+    for t in range(4):
+        nc.vector.scalar_tensor_tensor(out=ww[:, t, :], in0=xc[:, t, :], scalar=prm[t]["a1p"],
+                                       in1=kk[:, t, :], op0=ALU.mult, op1=ALU.subtract)
+    for t in range(4):
+        nc.scalar.activation(out=ww[:, t, :], in_=ww[:, t, :], func=AF.Sin, bias=prm[t]["sb"], scale=TWO_PI)
+    for t in range(4):
+        nc.vector.tensor_scalar(out=ll[:, t, :], in0=xc[:, t, :], scalar1=prm[t]["a3"],
+                                scalar2=prm[t]["c4"], op0=ALU.mult, op1=ALU.add)
+    for t in range(4):
+        nc.vector.scalar_tensor_tensor(out=tt[:, t, :], in0=tt[:, t, :], scalar=prm[t]["a0"],
+                                       in1=ww[:, t, :], op0=ALU.mult, op1=ALU.mult)
+    if permute:
+        nc.vector.tensor_tensor(out=out_ap, in0=tt[:].rearrange("q t b -> q b t"),
+                                in1=ll[:].rearrange("q t b -> q b t"), op=ALU.add)
+    else:
+        nc.vector.tensor_tensor(out=out_ap, in0=tt[:], in1=ll[:], op=ALU.add)
+
+
+def tile_network_w_kernel(tc, data, W1, b1, a1, W2_words, W2_scales, b2, a2,
+                                     W3_words, W3_scales, b3, a3, out):
+    nc = tc.nc
+    with ExitStack() as ctx:
+        const = ctx.enter_context(tc.tile_pool(name="const", bufs=1))
+        wts = ctx.enter_context(tc.tile_pool(name="wts", bufs=8))
+        work = ctx.enter_context(tc.tile_pool(name="work", bufs=3))
+        ps_a = ctx.enter_context(tc.psum_pool(name="ps_a", bufs=4))
+        ps_b = ctx.enter_context(tc.psum_pool(name="ps_b", bufs=4))
+
+        warm = const.tile([P, 1], F32, name="warm")
+        nc.vector.memset(warm[:], 0.0)
+        nc.scalar.activation(out=warm[:], in_=warm[:], func=AF.Silu)
+
+        praw = const.tile([P, 3072], BF16, name="praw")
+        p3raw = const.tile([P, 768], BF16, name="p3raw")
+        nc.vector.memset(praw[:], 0.0)
+        nc.vector.memset(p3raw[:], 0.0)
+        w2s = const.tile([P, 4096], U8, name="w2s", align_bytes=64)
+        w3s = const.tile([P, 2, 2048], U8, name="w3s", align_bytes=64)
+        nc.vector.memset(w2s[:].bitcast(I32), 0)
+        nc.vector.memset(w3s[:].rearrange("p a n -> p (a n)").bitcast(I32), 0)
+
+        ident_b = const.tile([P, P], BF16, name="ident_b")
+        make_identity(nc, ident_b[:])
+        ident_f = const.tile([P, P], F32, name="ident_f")
+        make_identity(nc, ident_f[:])
+
+        data_sb = const.tile([P, 2048], BF16, name="data_sb")
+        nc.sync.dma_start(out=data_sb[:], in_=data)
+
+        nc.scalar.dma_start(out=praw[0:4, 0:2560], in_=a1.rearrange("(g r) i -> g (r i)", g=4))
+        nc.scalar.dma_start(out=praw[0:4, 2560:3072], in_=b1.rearrange("(g r) -> g r", g=4))
+        nc.scalar.dma_start(out=praw[4:12, 0:2560], in_=a2.rearrange("(g r) i -> g (r i)", g=8))
+        nc.scalar.dma_start(out=praw[4:12, 2560:3072], in_=b2.rearrange("(g r) -> g r", g=8))
+        nc.scalar.dma_start(out=p3raw[0:16, 0:640], in_=a3.rearrange("(j r) i -> j (r i)", j=16))
+        nc.scalar.dma_start(out=p3raw[0:16, 640:768], in_=b3.rearrange("(j r) -> j r", j=16))
+
+        w1v = W1.rearrange("(j p) n -> p j n", p=P)
+        w1t = {}
+        for h in range(2):
+            for jc in range(4):
+                w = wts.tile([P, 4, 1024], BF16, name="w1_%d_%d" % (h, jc), tag="wA", align_bytes=64)
+                nc.sync.dma_start(out=w[:], in_=w1v[:, 4 * jc:4 * jc + 4, 1024 * h:1024 * h + 1024])
+                w1t[(h, jc)] = w
+
+        for q in range(4):
+            nc.sync.dma_start(out=w2s[32 * q:32 * q + 16, :].bitcast(I32),
+                              in_=W2_scales[:, 4 * q:4 * q + 4, :].bitcast(I32))
+        w2t = {}
+        for hh in range(2):
+            for g in range(4):
+                w = wts.tile([P, 2048], U32, name="w2_%d_%d" % (hh, g), tag="wB", align_bytes=64)
+                src = W2_words[g].rearrange("p n t -> p (n t)")[:, 8192 * hh:8192 * hh + 8192]
+                nc.sync.dma_start(out=w[:].bitcast(I32), in_=src.bitcast(I32))
+                w2t[(hh, g)] = w
+
+        for a in range(2):
+            for q in range(4):
+                nc.sync.dma_start(out=w3s[32 * q:32 * q + 16, a, :].bitcast(I32),
+                                  in_=W3_scales[4 * a:4 * a + 4, 4 * q:4 * q + 4, :].bitcast(I32))
+        w3_parts = [(0, 1024, 2), (1024, 512, 4), (1536, 512, 4)]
+        w3t = {}
+        for n0, ncol, gper in w3_parts:
+            for gc in range(8 // gper):
+                w = wts.tile([P, gper, ncol], U32, name="w3_%d_%d" % (n0, gc), tag="wA", align_bytes=64)
+                src = W3_words[gper * gc:gper * gc + gper].rearrange("g p n t -> p g (n t)")
+                nc.sync.dma_start(out=w[:].bitcast(I32), in_=src[:, :, 4 * n0:4 * (n0 + ncol)].bitcast(I32))
+                for gi in range(gper):
+                    for j in range(n0 // P, (n0 + ncol) // P):
+                        w3t[(j, gper * gc + gi)] = w[:, gi, P * j - n0:P * j - n0 + P]
+
+        dataT = const.tile([P, 16, P], BF16, name="dataT")
+        for half in range(2):
+            dps = ps_b.tile([P, 8, P], BF16, name="dps_%d" % half, tag="xt")
+            for jj in range(8):
+                j = 8 * half + jj
+                nc.tensor.transpose(out=dps[:, jj, :], in_=data_sb[:, P * j:P * j + P], identity=ident_b[:])
+            if half == 0:
+                nc.vector.tensor_copy(out=dataT[:, 0:8, :], in_=dps[:])
+            else:
+                nc.scalar.copy(out=dataT[:, 8:16, :], in_=dps[:])
+
+        praw_w = praw[:].bitcast(F32)
+        pde = const.tile([P, 12, P], F32, name="pde")
+        nc.vector.tensor_copy(out=pde[:, 0:10, :], in_=praw_w[:, 0:1280].rearrange("r (p w) -> r w p", w=10))
+        nc.vector.tensor_copy(out=pde[:, 10:12, :], in_=praw_w[:, 1280:1536].rearrange("r (p w) -> r w p", w=2))
+        par = const.tile([P, 24, 12], F32, name="par")
+        for wb in range(3):
+            pp = ps_b.tile([P, 4, P], F32, name="pp_%d" % wb, tag="xt")
+            for wi in range(4):
+                nc.tensor.transpose(out=pp[:, wi, :], in_=pde[:, 4 * wb + wi, :], identity=ident_f[:])
+            nc.vector.tensor_copy(
+                out=par[:, 8 * wb:8 * wb + 8, :].rearrange("p (w e) r -> p w r e", e=2),
+                in_=pp[:].bitcast(BF16)[:, :, 0:24].rearrange("p w (r e) -> p w r e", e=2))
+        der = const.tile([P, 4, 4, 12], F32, name="der")
+        derive(nc, [par[:, i:20:5, :] for i in range(5)], par[:, 20:24, :], [der[:, i, :, :] for i in range(4)])
+
+        def prm12(r):
+            return [{"b": par[:, 20 + t, r:r + 1], "a0": par[:, 5 * t, r:r + 1], "a3": par[:, 5 * t + 3, r:r + 1],
+                     "a1p": der[:, 0, t, r:r + 1], "sb": der[:, 1, t, r:r + 1], "c2p": der[:, 2, t, r:r + 1],
+                     "c4": der[:, 3, t, r:r + 1]} for t in range(4)]
+
+        def to_nodes(acc, label):
+            xs = work.tile([P, 4, P], F32, name="xs_" + label, tag="xs")
+            nc.scalar.copy(out=xs[:], in_=acc[:].rearrange("b (q t) -> b t q", t=4))
+            xt = ps_b.tile([P, 4, P], F32, name="xt_" + label, tag="xt")
+            for t in range(4):
+                nc.tensor.transpose(out=xt[:, t, :], in_=xs[:, t, :], identity=ident_f[:])
+            xc = work.tile([P, 4, P], F32, name="xc_" + label, tag="xc")
+            nc.scalar.copy(out=xc[:], in_=xt[:])
+            return xc
+
+        hb1 = const.tile([P, 4, P, 4], BF16, name="hb1", align_bytes=64)
+        h1w = const.tile([P, 4, P], U32, name="h1w", align_bytes=64)
+        h1s = const.tile([P, 4, P], U8, name="h1s", align_bytes=64)
+        for h in range(2):
+            accs = [ps_a.tile([P, 512], F32, name="acc1_%d_%d" % (h, nb), tag="acc") for nb in range(2)]
+            for j in range(16):
+                for nb in range(2):
+                    nc.tensor.matmul(out=accs[nb][:], lhsT=dataT[:, j, :],
+                                     rhs=w1t[(h, j // 4)][:, j % 4, 512 * nb:512 * nb + 512],
+                                     start=(j == 0), stop=(j == 15))
+            for nb in range(2):
+                g = 2 * h + nb
+                xc = to_nodes(accs[nb], "l1_%d" % g)
+                node_act(nc, work, xc, prm12(g), hb1[:, g, :, :], True, "l1_%d" % g)
+                nc.vector.quantize_mx(out=h1w[:, g, :].bitcast(FP8X4), scales=h1s[:, g, :],
+                                      in_=hb1[:, g, :, :].rearrange("q b t -> q (b t)"))
+
+        p3de = const.tile([P, 5, P], BF16, name="p3de")
+        nc.vector.tensor_copy(out=p3de[:], in_=p3raw[:, 0:640].rearrange("r (p c) -> r c p", c=5))
+        pp3 = ps_b.tile([P, 8, P], BF16, name="pp3", tag="xt")
+        for i in range(5):
+            nc.tensor.transpose(out=pp3[:, i, :], in_=p3de[:, i, :], identity=ident_b[:])
+        nc.tensor.transpose(out=pp3[:, 5, :], in_=p3raw[:, 640:768], identity=ident_b[:])
+        par3 = const.tile([P, 6, 16], F32, name="par3")
+        nc.vector.tensor_copy(out=par3[:], in_=pp3[:, 0:6, 0:16])
+        der3 = const.tile([P, 4, 16], F32, name="der3")
+        derive(nc, [par3[:, i, :] for i in range(5)], par3[:, 5, :], [der3[:, i, :] for i in range(4)])
+
+        def prm3(jb):
+            return [{"b": par3[:, 5, j:j + 1], "a0": par3[:, 0, j:j + 1], "a3": par3[:, 3, j:j + 1],
+                     "a1p": der3[:, 0, j:j + 1], "sb": der3[:, 1, j:j + 1], "c2p": der3[:, 2, j:j + 1],
+                     "c4": der3[:, 3, j:j + 1]} for j in range(4 * jb, 4 * jb + 4)]
+
+        hb2 = const.tile([P, 8, P, 4], BF16, name="hb2", align_bytes=64)
+        h2w = const.tile([P, 8, P], U32, name="h2w", align_bytes=64)
+        h2s = const.tile([P, 8, P], U8, name="h2s", align_bytes=64)
+        for c in range(8):
+            acc = ps_a.tile([P, 512], F32, name="acc2_%d" % c, tag="acc")
+            for g in range(4):
+                nc.tensor.matmul_mx(out=acc[:], lhsT=h1w[:, g, :].bitcast(FP8X4), lhsT_scale=h1s[:, g, :],
+                                    rhs=w2t[(c // 4, g)][:, 512 * (c % 4):512 * (c % 4) + 512].bitcast(FP8X4),
+                                    rhs_scale=w2s[4 * g:P, 512 * c:512 * c + 512],
+                                    start=(g == 0), stop=(g == 3))
+            xc = to_nodes(acc, "l2_%d" % c)
+            node_act(nc, work, xc, prm12(4 + c), hb2[:, c, :, :], True, "l2_%d" % c)
+            nc.vector.quantize_mx(out=h2w[:, c, :].bitcast(FP8X4), scales=h2s[:, c, :],
+                                  in_=hb2[:, c, :, :].rearrange("q b t -> q (b t)"))
+
+        m4 = const.tile([P, 4], F32, name="m4")
+        hts = []
+        for jb in range(4):
+            acc = ps_a.tile([P, 4, P], F32, name="acc3_%d" % jb, tag="acc")
+            for jj in range(4):
+                j = 4 * jb + jj
+                for g in range(8):
+                    nc.tensor.matmul_mx(out=acc[:, jj, :], lhsT=w3t[(j, g)].bitcast(FP8X4),
+                                        lhsT_scale=w3s[4 * (g % 4):P, g // 4, P * j:P * j + P],
+                                        rhs=h2w[:, g, :].bitcast(FP8X4), rhs_scale=h2s[:, g, :],
+                                        start=(g == 0), stop=(g == 7))
+            xc = work.tile([P, 4, P], F32, name="xc_l3_%d" % jb, tag="xc")
+            nc.scalar.copy(out=xc[:], in_=acc[:])
+            h3 = work.tile([P, 4, P], F32, name="h3_%d" % jb, tag="xs")
+            node_act(nc, work, xc, prm3(jb), h3[:], False, "l3_%d" % jb)
+            ht = ps_b.tile([P, 4, P], F32, name="ht_%d" % jb, tag="xt")
+            for jj in range(4):
+                nc.tensor.transpose(out=ht[:, jj, :], in_=h3[:, jj, :], identity=ident_f[:])
+            nc.vector.reduce_max(out=m4[:, jb:jb + 1], in_=ht[:].rearrange("b j n -> b (j n)"), axis=AX.X)
+            hts.append(ht)
+
+        negm = const.tile([P, 1], F32, name="negm")
+        nc.vector.reduce_max(out=negm[:], in_=m4[:], axis=AX.X)
+        nc.vector.tensor_scalar(out=negm[:], in0=negm[:], scalar1=-1.0, scalar2=None, op0=ALU.mult)
+        ee = const.tile([P, 4, 512], F32, name="ee")
+        s4 = const.tile([P, 4], F32, name="s4")
+        for jb in range(4):
+            nc.scalar.activation(out=ee[:, jb, :], in_=hts[jb][:].rearrange("b j n -> b (j n)"), func=AF.Exp,
+                                 bias=negm[:, 0:1], scale=1.0, accum_out=s4[:, jb:jb + 1])
+        rs = const.tile([P, 1], F32, name="rs")
+        nc.vector.reduce_sum(out=rs[:], in_=s4[:], axis=AX.X)
+        nc.vector.reciprocal(out=rs[:], in_=rs[:])
+        for jb in range(4):
+            if jb % 2 == 0:
+                nc.vector.tensor_scalar(out=ee[:, jb, :], in0=ee[:, jb, :], scalar1=rs[:, 0:1], scalar2=None,
+                                        op0=ALU.mult)
+            else:
+                nc.scalar.activation(out=ee[:, jb, :], in_=ee[:, jb, :], func=AF.Copy, scale=rs[:, 0:1])
+            nc.sync.dma_start(out=out[:, 512 * jb:512 * jb + 512], in_=ee[:, jb, :])

@@ -29,34 +29,6 @@ def derive(nc, a, bb, d):
     nc.vector.tensor_tensor(out=d[3], in0=d[3], in1=a[4], op=ALU.add)
 
 
-def node_act(nc, work, xc, prm, out_ap, permute, label):
-    kk = work.tile([P, 4, P], I32, name="kk_" + label, tag="kk")
-    tt = work.tile([P, 4, P], F32, name="tt_" + label, tag="tt")
-    ww = work.tile([P, 4, P], F32, name="ww_" + label, tag="ww")
-    ll = work.tile([P, 4, P], F32, name="ll_" + label, tag="ll")
-    for t in range(4):
-        nc.vector.tensor_scalar(out=kk[:, t, :], in0=xc[:, t, :], scalar1=prm[t]["a1p"],
-                                scalar2=prm[t]["c2p"], op0=ALU.mult, op1=ALU.add)
-    for t in range(4):
-        nc.scalar.activation(out=tt[:, t, :], in_=xc[:, t, :], func=AF.Tanh, bias=prm[t]["b"], scale=1.0)
-    for t in range(4):
-        nc.vector.scalar_tensor_tensor(out=ww[:, t, :], in0=xc[:, t, :], scalar=prm[t]["a1p"],
-                                       in1=kk[:, t, :], op0=ALU.mult, op1=ALU.subtract)
-    for t in range(4):
-        nc.scalar.activation(out=ww[:, t, :], in_=ww[:, t, :], func=AF.Sin, bias=prm[t]["sb"], scale=TWO_PI)
-    for t in range(4):
-        nc.vector.tensor_scalar(out=ll[:, t, :], in0=xc[:, t, :], scalar1=prm[t]["a3"],
-                                scalar2=prm[t]["c4"], op0=ALU.mult, op1=ALU.add)
-    for t in range(4):
-        nc.vector.scalar_tensor_tensor(out=tt[:, t, :], in0=tt[:, t, :], scalar=prm[t]["a0"],
-                                       in1=ww[:, t, :], op0=ALU.mult, op1=ALU.mult)
-    if permute:
-        nc.vector.tensor_tensor(out=out_ap, in0=tt[:].rearrange("q t b -> q b t"),
-                                in1=ll[:].rearrange("q t b -> q b t"), op=ALU.add)
-    else:
-        nc.vector.tensor_tensor(out=out_ap, in0=tt[:], in1=ll[:], op=ALU.add)
-
-
 def tile_network_w_kernel(tc, data, W1, b1, a1, W2_words, W2_scales, b2, a2,
                                      W3_words, W3_scales, b3, a3, out):
     nc = tc.nc
@@ -64,8 +36,8 @@ def tile_network_w_kernel(tc, data, W1, b1, a1, W2_words, W2_scales, b2, a2,
         const = ctx.enter_context(tc.tile_pool(name="const", bufs=1))
         wts = ctx.enter_context(tc.tile_pool(name="wts", bufs=8))
         work = ctx.enter_context(tc.tile_pool(name="work", bufs=3))
-        ps_a = ctx.enter_context(tc.psum_pool(name="ps_a", bufs=4))
-        ps_b = ctx.enter_context(tc.psum_pool(name="ps_b", bufs=4))
+        psum = ctx.enter_context(tc.psum_pool(name="psum", bufs=1))
+        ctx.enter_context(tc.manual_schedule())
 
         warm = const.tile([P, 1], F32, name="warm")
         nc.vector.memset(warm[:], 0.0)
@@ -97,11 +69,18 @@ def tile_network_w_kernel(tc, data, W1, b1, a1, W2_words, W2_scales, b2, a2,
 
         w1v = W1.rearrange("(j p) n -> p j n", p=P)
         w1t = {}
-        for h in range(2):
-            for jc in range(4):
-                w = wts.tile([P, 4, 1024], BF16, name="w1_%d_%d" % (h, jc), tag="wA", align_bytes=64)
-                nc.sync.dma_start(out=w[:], in_=w1v[:, 4 * jc:4 * jc + 4, 1024 * h:1024 * h + 1024])
-                w1t[(h, jc)] = w
+        for jc in range(4):
+            w = wts.tile([P, 4, 1024], BF16, name="w1_h_%d" % jc, tag="wA", align_bytes=64)
+            nc.sync.dma_start(out=w[:], in_=w1v[:, 4 * jc:4 * jc + 4, 0:1024])
+            for jj in range(4):
+                for nb in range(2):
+                    w1t[(nb, 4 * jc + jj)] = w[:, jj, 512 * nb:512 * nb + 512]
+        for g in range(2, 4):
+            for jc in range(2):
+                w = wts.tile([P, 8, 512], BF16, name="w1_q%d_%d" % (g, jc), tag="wA", align_bytes=64)
+                nc.sync.dma_start(out=w[:], in_=w1v[:, 8 * jc:8 * jc + 8, 512 * g:512 * g + 512])
+                for jj in range(8):
+                    w1t[(g, 8 * jc + jj)] = w[:, jj, :]
 
         for q in range(4):
             nc.sync.dma_start(out=w2s[32 * q:32 * q + 16, :].bitcast(I32),
@@ -129,24 +108,31 @@ def tile_network_w_kernel(tc, data, W1, b1, a1, W2_words, W2_scales, b2, a2,
                     for j in range(n0 // P, (n0 + ncol) // P):
                         w3t[(j, gper * gc + gi)] = w[:, gi, P * j - n0:P * j - n0 + P]
 
-        dataT = const.tile([P, 16, P], BF16, name="dataT")
-        for half in range(2):
-            dps = ps_b.tile([P, 8, P], BF16, name="dps_%d" % half, tag="xt")
-            for jj in range(8):
-                j = 8 * half + jj
-                nc.tensor.transpose(out=dps[:, jj, :], in_=data_sb[:, P * j:P * j + P], identity=ident_b[:])
-            if half == 0:
-                nc.vector.tensor_copy(out=dataT[:, 0:8, :], in_=dps[:])
-            else:
-                nc.scalar.copy(out=dataT[:, 8:16, :], in_=dps[:])
-
         praw_w = praw[:].bitcast(F32)
         pde = const.tile([P, 12, P], F32, name="pde")
         nc.vector.tensor_copy(out=pde[:, 0:10, :], in_=praw_w[:, 0:1280].rearrange("r (p w) -> r w p", w=10))
         nc.vector.tensor_copy(out=pde[:, 10:12, :], in_=praw_w[:, 1280:1536].rearrange("r (p w) -> r w p", w=2))
+        p3de = const.tile([P, 5, P], BF16, name="p3de")
+        nc.vector.tensor_copy(out=p3de[:], in_=p3raw[:, 0:640].rearrange("r (p c) -> r c p", c=5))
+
+        dataT = const.tile([P, 16, P], BF16, name="dataT")
+        for half in range(2):
+            dps = psum.tile([P, 8, P], BF16, name="dps_%d" % half, tag=("x0d", "x0a")[half])
+            for jj in range(8):
+                j = 8 * half + jj
+                nc.tensor.transpose(out=dps[:, jj, :], in_=data_sb[:, P * j:P * j + P], identity=ident_b[:])
+            nc.scalar.copy(out=dataT[:, 8 * half:8 * half + 8, :], in_=dps[:])
+
+        pp3 = psum.tile([P, 8, P], BF16, name="pp3", tag="x1d")
+        for i in range(5):
+            nc.tensor.transpose(out=pp3[:, i, :], in_=p3de[:, i, :], identity=ident_b[:])
+        nc.tensor.transpose(out=pp3[:, 5, :], in_=p3raw[:, 640:768], identity=ident_b[:])
+        par3 = const.tile([P, 6, 16], F32, name="par3")
+        nc.vector.tensor_copy(out=par3[:], in_=pp3[:, 0:6, 0:16])
+
         par = const.tile([P, 24, 12], F32, name="par")
         for wb in range(3):
-            pp = ps_b.tile([P, 4, P], F32, name="pp_%d" % wb, tag="xt")
+            pp = psum.tile([P, 4, P], F32, name="pp_%d" % wb, tag=("x1a", "x0d", "x0a")[wb])
             for wi in range(4):
                 nc.tensor.transpose(out=pp[:, wi, :], in_=pde[:, 4 * wb + wi, :], identity=ident_f[:])
             nc.vector.tensor_copy(
@@ -154,106 +140,277 @@ def tile_network_w_kernel(tc, data, W1, b1, a1, W2_words, W2_scales, b2, a2,
                 in_=pp[:].bitcast(BF16)[:, :, 0:24].rearrange("p w (r e) -> p w r e", e=2))
         der = const.tile([P, 4, 4, 12], F32, name="der")
         derive(nc, [par[:, i:20:5, :] for i in range(5)], par[:, 20:24, :], [der[:, i, :, :] for i in range(4)])
+        der3 = const.tile([P, 4, 16], F32, name="der3")
+        derive(nc, [par3[:, i, :] for i in range(5)], par3[:, 5, :], [der3[:, i, :] for i in range(4)])
 
-        def prm12(r):
-            return [{"b": par[:, 20 + t, r:r + 1], "a0": par[:, 5 * t, r:r + 1], "a3": par[:, 5 * t + 3, r:r + 1],
-                     "a1p": der[:, 0, t, r:r + 1], "sb": der[:, 1, t, r:r + 1], "c2p": der[:, 2, t, r:r + 1],
-                     "c4": der[:, 3, t, r:r + 1]} for t in range(4)]
-
-        def to_nodes(acc, label):
-            xs = work.tile([P, 4, P], F32, name="xs_" + label, tag="xs")
-            nc.scalar.copy(out=xs[:], in_=acc[:].rearrange("b (q t) -> b t q", t=4))
-            xt = ps_b.tile([P, 4, P], F32, name="xt_" + label, tag="xt")
-            for t in range(4):
-                nc.tensor.transpose(out=xt[:, t, :], in_=xs[:, t, :], identity=ident_f[:])
-            xc = work.tile([P, 4, P], F32, name="xc_" + label, tag="xc")
-            nc.scalar.copy(out=xc[:], in_=xt[:])
-            return xc
+        def prm(i):
+            if i < 12:
+                return [{"b": par[:, 20 + t, i:i + 1], "a0": par[:, 5 * t, i:i + 1], "a3": par[:, 5 * t + 3, i:i + 1],
+                         "a1p": der[:, 0, t, i:i + 1], "sb": der[:, 1, t, i:i + 1], "c2p": der[:, 2, t, i:i + 1],
+                         "c4": der[:, 3, t, i:i + 1]} for t in range(4)]
+            return [{"b": par3[:, 5, j:j + 1], "a0": par3[:, 0, j:j + 1], "a3": par3[:, 3, j:j + 1],
+                     "a1p": der3[:, 0, j:j + 1], "sb": der3[:, 1, j:j + 1], "c2p": der3[:, 2, j:j + 1],
+                     "c4": der3[:, 3, j:j + 1]} for j in range(4 * (i - 12), 4 * (i - 12) + 4)]
 
         hb1 = const.tile([P, 4, P, 4], BF16, name="hb1", align_bytes=64)
         h1w = const.tile([P, 4, P], U32, name="h1w", align_bytes=64)
         h1s = const.tile([P, 4, P], U8, name="h1s", align_bytes=64)
-        for h in range(2):
-            accs = [ps_a.tile([P, 512], F32, name="acc1_%d_%d" % (h, nb), tag="acc") for nb in range(2)]
-            for j in range(16):
-                for nb in range(2):
-                    nc.tensor.matmul(out=accs[nb][:], lhsT=dataT[:, j, :],
-                                     rhs=w1t[(h, j // 4)][:, j % 4, 512 * nb:512 * nb + 512],
-                                     start=(j == 0), stop=(j == 15))
-            for nb in range(2):
-                g = 2 * h + nb
-                xc = to_nodes(accs[nb], "l1_%d" % g)
-                node_act(nc, work, xc, prm12(g), hb1[:, g, :, :], True, "l1_%d" % g)
-                nc.vector.quantize_mx(out=h1w[:, g, :].bitcast(FP8X4), scales=h1s[:, g, :],
-                                      in_=hb1[:, g, :, :].rearrange("q b t -> q (b t)"))
-
-        p3de = const.tile([P, 5, P], BF16, name="p3de")
-        nc.vector.tensor_copy(out=p3de[:], in_=p3raw[:, 0:640].rearrange("r (p c) -> r c p", c=5))
-        pp3 = ps_b.tile([P, 8, P], BF16, name="pp3", tag="xt")
-        for i in range(5):
-            nc.tensor.transpose(out=pp3[:, i, :], in_=p3de[:, i, :], identity=ident_b[:])
-        nc.tensor.transpose(out=pp3[:, 5, :], in_=p3raw[:, 640:768], identity=ident_b[:])
-        par3 = const.tile([P, 6, 16], F32, name="par3")
-        nc.vector.tensor_copy(out=par3[:], in_=pp3[:, 0:6, 0:16])
-        der3 = const.tile([P, 4, 16], F32, name="der3")
-        derive(nc, [par3[:, i, :] for i in range(5)], par3[:, 5, :], [der3[:, i, :] for i in range(4)])
-
-        def prm3(jb):
-            return [{"b": par3[:, 5, j:j + 1], "a0": par3[:, 0, j:j + 1], "a3": par3[:, 3, j:j + 1],
-                     "a1p": der3[:, 0, j:j + 1], "sb": der3[:, 1, j:j + 1], "c2p": der3[:, 2, j:j + 1],
-                     "c4": der3[:, 3, j:j + 1]} for j in range(4 * jb, 4 * jb + 4)]
-
         hb2 = const.tile([P, 8, P, 4], BF16, name="hb2", align_bytes=64)
         h2w = const.tile([P, 8, P], U32, name="h2w", align_bytes=64)
         h2s = const.tile([P, 8, P], U8, name="h2s", align_bytes=64)
-        for c in range(8):
-            acc = ps_a.tile([P, 512], F32, name="acc2_%d" % c, tag="acc")
-            for g in range(4):
-                nc.tensor.matmul_mx(out=acc[:], lhsT=h1w[:, g, :].bitcast(FP8X4), lhsT_scale=h1s[:, g, :],
-                                    rhs=w2t[(c // 4, g)][:, 512 * (c % 4):512 * (c % 4) + 512].bitcast(FP8X4),
-                                    rhs_scale=w2s[4 * g:P, 512 * c:512 * c + 512],
-                                    start=(g == 0), stop=(g == 3))
-            xc = to_nodes(acc, "l2_%d" % c)
-            node_act(nc, work, xc, prm12(4 + c), hb2[:, c, :, :], True, "l2_%d" % c)
-            nc.vector.quantize_mx(out=h2w[:, c, :].bitcast(FP8X4), scales=h2s[:, c, :],
-                                  in_=hb2[:, c, :, :].rearrange("q b t -> q (b t)"))
+
+        st = {}
+
+        def ev(i, acc):
+            xs = work.tile([P, 4, P], F32, name="xs%d" % i, tag="xs")
+            nc.scalar.copy(out=xs[:], in_=acc[:].rearrange("b (q t) -> b t q", t=4))
+            st[("xs", i)] = xs
+
+        def tr(i, both):
+            for kind in (("d", "a") if both else ("d",)):
+                xt = psum.tile([P, 4, P], F32, name="xt%s%d" % (kind, i), tag="x%d%s" % (i % 2, kind))
+                for t in range(4):
+                    nc.tensor.transpose(out=xt[:, t, :], in_=st[("xs", i)][:, t, :], identity=ident_f[:])
+                st[("x" + kind, i)] = xt
+
+        def cp(i):
+            xc = work.tile([P, 4, P], F32, name="xc%d" % i, tag="xc")
+            nc.scalar.copy(out=xc[:], in_=st[("xd", i)][:])
+            st[("xd", i)] = xc
+            st[("xa", i)] = xc
+
+        def ab(i):
+            kk = work.tile([P, 4, P], I32, name="kk%d" % i, tag="kk")
+            ww = work.tile([P, 4, P], F32, name="ww%d" % i, tag="ww")
+            x = st[("xd", i)]
+            pr = prm(i)
+            for t in range(4):
+                nc.vector.tensor_scalar(out=kk[:, t, :], in0=x[:, t, :], scalar1=pr[t]["a1p"],
+                                        scalar2=pr[t]["c2p"], op0=ALU.mult, op1=ALU.add)
+            for t in range(4):
+                nc.vector.scalar_tensor_tensor(out=ww[:, t, :], in0=x[:, t, :], scalar=pr[t]["a1p"],
+                                               in1=kk[:, t, :], op0=ALU.mult, op1=ALU.subtract)
+            st[("ww", i)] = ww
+
+        def th(i):
+            tt = work.tile([P, 4, P], F32, name="tt%d" % i, tag="tt")
+            x = st[("xa", i)]
+            pr = prm(i)
+            for t in range(4):
+                nc.scalar.activation(out=tt[:, t, :], in_=x[:, t, :], func=AF.Tanh, bias=pr[t]["b"], scale=1.0)
+            st[("tt", i)] = tt
+
+        def sn(i):
+            ww = st[("ww", i)]
+            pr = prm(i)
+            for t in range(4):
+                nc.scalar.activation(out=ww[:, t, :], in_=ww[:, t, :], func=AF.Sin, bias=pr[t]["sb"], scale=TWO_PI)
+
+        def lin(i, on_scalar):
+            ll = work.tile([P, 4, P], F32, name="ll%d" % i, tag="ll")
+            pr = prm(i)
+            for t in range(4):
+                if on_scalar:
+                    nc.scalar.activation(out=ll[:, t, :], in_=st[("xa", i)][:, t, :], func=AF.Identity,
+                                         bias=pr[t]["c4"], scale=pr[t]["a3"])
+                else:
+                    nc.vector.tensor_scalar(out=ll[:, t, :], in0=st[("xd", i)][:, t, :], scalar1=pr[t]["a3"],
+                                            scalar2=pr[t]["c4"], op0=ALU.mult, op1=ALU.add)
+            st[("ll", i)] = ll
+
+        def pm(i):
+            tt = st[("tt", i)]
+            pr = prm(i)
+            for t in range(4):
+                nc.vector.scalar_tensor_tensor(out=tt[:, t, :], in0=tt[:, t, :], scalar=pr[t]["a0"],
+                                               in1=st[("ww", i)][:, t, :], op0=ALU.mult, op1=ALU.mult)
+
+        def hq(i):
+            hb, hw, hs, g = (hb1, h1w, h1s, i) if i < 4 else (hb2, h2w, h2s, i - 4)
+            nc.vector.tensor_tensor(out=hb[:, g, :, :], in0=st[("tt", i)][:].rearrange("q t b -> q b t"),
+                                    in1=st[("ll", i)][:].rearrange("q t b -> q b t"), op=ALU.add)
+            nc.vector.quantize_mx(out=hw[:, g, :].bitcast(FP8X4), scales=hs[:, g, :],
+                                  in_=hb[:, g, :, :].rearrange("q b t -> q (b t)"))
+
+        acc1 = {}
+
+        def l1_mm(pairs):
+            for g, j in pairs:
+                if j == 0:
+                    acc1[g] = psum.tile([P, 512], F32, name="acc1_%d" % g, tag="a%d" % g)
+                nc.tensor.matmul(out=acc1[g][:], lhsT=dataT[:, j, :], rhs=w1t[(g, j)],
+                                 start=(j == 0), stop=(j == 15))
+
+        acc2 = {}
+
+        def mx2(c, g):
+            if g == 0:
+                acc2[c] = psum.tile([P, 512], F32, name="acc2_%d" % c, tag="a%d" % (c % 4))
+            nc.tensor.matmul_mx(out=acc2[c][:], lhsT=h1w[:, g, :].bitcast(FP8X4), lhsT_scale=h1s[:, g, :],
+                                rhs=w2t[(c // 4, g)][:, 512 * (c % 4):512 * (c % 4) + 512].bitcast(FP8X4),
+                                rhs_scale=w2s[4 * g:P, 512 * c:512 * c + 512],
+                                start=(g == 0), stop=(g == 3))
+
+        x3 = {}
+        x3_bank = {0: "a0", 1: "a1", 2: "a2", 3: "a3", 4: "x0d", 5: "x0a", 6: "x1d", 7: "x1a"}
+
+        def mx3(j, g):
+            if g == 0:
+                if j < 8:
+                    x3[j] = psum.tile([P, P], F32, name="x3_%d" % j, tag=x3_bank[j])[:]
+                elif j % 4 == 0:
+                    big = psum.tile([P, 4, P], F32, name="x3_%d" % j, tag=("a1" if j == 8 else "a2"))
+                    for jj in range(4):
+                        x3[j + jj] = big[:, jj, :]
+            nc.tensor.matmul_mx(out=x3[j], lhsT=w3t[(j, g)].bitcast(FP8X4),
+                                lhsT_scale=w3s[4 * (g % 4):P, g // 4, P * j:P * j + P],
+                                rhs=h2w[:, g, :].bitcast(FP8X4), rhs_scale=h2s[:, g, :],
+                                start=(g == 0), stop=(g == 7))
+
+        l1_mm([(g, j) for j in range(12) for g in range(2)])
+        l1_mm([(g, j) for g in range(2) for j in range(12, 16)])
+        ev(0, acc1[0])
+        ev(1, acc1[1])
+        l1_mm([(2, j) for j in range(8)])
+        tr(0, False)
+        tr(1, False)
+        l1_mm([(2, j) for j in range(8, 16)])
+        l1_mm([(3, j) for j in range(8)])
+        for i in range(3):
+            cp(i)
+            ab(i)
+            th(i)
+            lin(i, False)
+            if i == 1:
+                ev(2, acc1[2])
+                tr(2, False)
+                l1_mm([(3, j) for j in range(8, 16)])
+            sn(i)
+            pm(i)
+            hq(i)
+        ev(3, acc1[3])
+        tr(3, True)
+        for g in range(3):
+            for c in range(4):
+                mx2(c, g)
+        ab(3)
+        th(3)
+        lin(3, False)
+        sn(3)
+        pm(3)
+        hq(3)
+        for c in range(4):
+            mx2(c, 3)
+
+        ev(4, acc2[0])
+        tr(4, True)
+        for i in range(4, 12):
+            c = i - 4
+            if c < 7:
+                ev(i + 1, acc2[c + 1])
+                tr(i + 1, True)
+            if 4 <= c + 2 < 8:
+                for g in range(4):
+                    mx2(c + 2, g)
+            if c == 6:
+                for g in range(5):
+                    for j in range(4):
+                        mx3(j, g)
+            if c == 7:
+                for j in range(4):
+                    mx3(j, 5)
+                for g in range(6):
+                    for j in range(4, 6):
+                        mx3(j, g)
+            ab(i)
+            th(i)
+            if c > 0:
+                hq(i - 1)
+            if c == 7:
+                lin(i, False)
+                sn(i)
+            else:
+                sn(i)
+                lin(i, True)
+            pm(i)
+        hq(11)
+        for g in range(6, 8):
+            for j in range(4):
+                mx3(j, g)
+        for g in range(6, 8):
+            for j in range(4, 6):
+                mx3(j, g)
+        for j in range(6, 8):
+            for g in range(8):
+                mx3(j, g)
 
         m4 = const.tile([P, 4], F32, name="m4")
-        hts = []
-        for jb in range(4):
-            acc = ps_a.tile([P, 4, P], F32, name="acc3_%d" % jb, tag="acc")
-            for jj in range(4):
-                j = 4 * jb + jj
-                for g in range(8):
-                    nc.tensor.matmul_mx(out=acc[:, jj, :], lhsT=w3t[(j, g)].bitcast(FP8X4),
-                                        lhsT_scale=w3s[4 * (g % 4):P, g // 4, P * j:P * j + P],
-                                        rhs=h2w[:, g, :].bitcast(FP8X4), rhs_scale=h2s[:, g, :],
-                                        start=(g == 0), stop=(g == 7))
-            xc = work.tile([P, 4, P], F32, name="xc_l3_%d" % jb, tag="xc")
-            nc.scalar.copy(out=xc[:], in_=acc[:])
-            h3 = work.tile([P, 4, P], F32, name="h3_%d" % jb, tag="xs")
-            node_act(nc, work, xc, prm3(jb), h3[:], False, "l3_%d" % jb)
-            ht = ps_b.tile([P, 4, P], F32, name="ht_%d" % jb, tag="xt")
-            for jj in range(4):
-                nc.tensor.transpose(out=ht[:, jj, :], in_=h3[:, jj, :], identity=ident_f[:])
-            nc.vector.reduce_max(out=m4[:, jb:jb + 1], in_=ht[:].rearrange("b j n -> b (j n)"), axis=AX.X)
-            hts.append(ht)
+        hts = {}
 
-        negm = const.tile([P, 1], F32, name="negm")
-        nc.vector.reduce_max(out=negm[:], in_=m4[:], axis=AX.X)
-        nc.vector.tensor_scalar(out=negm[:], in0=negm[:], scalar1=-1.0, scalar2=None, op0=ALU.mult)
-        ee = const.tile([P, 4, 512], F32, name="ee")
+        def cp3(k):
+            xc = work.tile([P, 4, P], F32, name="xc%d" % (12 + k), tag="xc")
+            for t in range(4):
+                nc.scalar.copy(out=xc[:, t, :], in_=x3[4 * k + t])
+            st[("xd", 12 + k)] = xc
+            st[("xa", 12 + k)] = xc
+
+        def h3(k, by_tile):
+            hh = work.tile([P, 4, P], F32, name="h3_%d" % k, tag="xs")
+            ht = psum.tile([P, 4, P], F32, name="ht_%d" % k, tag=("a0", "a3", "x0d", "x0a")[k])
+            tt, ll = st[("tt", 12 + k)], st[("ll", 12 + k)]
+            if not by_tile:
+                nc.vector.tensor_tensor(out=hh[:], in0=tt[:], in1=ll[:], op=ALU.add)
+            for t in range(4):
+                if by_tile:
+                    nc.vector.tensor_tensor(out=hh[:, t, :], in0=tt[:, t, :], in1=ll[:, t, :], op=ALU.add)
+                nc.tensor.transpose(out=ht[:, t, :], in_=hh[:, t, :], identity=ident_f[:])
+            hts[k] = ht
+
+        def rowmax(k):
+            nc.vector.reduce_max(out=m4[:, k:k + 1], in_=hts[k][:].rearrange("b j n -> b (j n)"), axis=AX.X)
+
+        cp3(0)
+        for j in range(8, 16):
+            for g in range(8):
+                mx3(j, g)
+        for k in range(4):
+            i = 12 + k
+            ab(i)
+            th(i)
+            if k >= 1:
+                h3(k - 1, False)
+            if k >= 2:
+                rowmax(k - 2)
+            sn(i)
+            if k < 3:
+                cp3(k + 1)
+            lin(i, True)
+            pm(i)
+        h3(3, True)
+
+        sm = const.tile([P, 8], F32, name="sm")
+        fac = const.tile([P, 1], F32, name="fac")
         s4 = const.tile([P, 4], F32, name="s4")
-        for jb in range(4):
-            nc.scalar.activation(out=ee[:, jb, :], in_=hts[jb][:].rearrange("b j n -> b (j n)"), func=AF.Exp,
-                                 bias=negm[:, 0:1], scale=1.0, accum_out=s4[:, jb:jb + 1])
-        rs = const.tile([P, 1], F32, name="rs")
-        nc.vector.reduce_sum(out=rs[:], in_=s4[:], axis=AX.X)
-        nc.vector.reciprocal(out=rs[:], in_=rs[:])
-        for jb in range(4):
-            if jb % 2 == 0:
-                nc.vector.tensor_scalar(out=ee[:, jb, :], in0=ee[:, jb, :], scalar1=rs[:, 0:1], scalar2=None,
-                                        op0=ALU.mult)
-            else:
-                nc.scalar.activation(out=ee[:, jb, :], in_=ee[:, jb, :], func=AF.Copy, scale=rs[:, 0:1])
-            nc.sync.dma_start(out=out[:, 512 * jb:512 * jb + 512], in_=ee[:, jb, :])
+        ee = const.tile([P, 4, 512], F32, name="ee")
+        m_a, neg_a, neg_f, s_a, tot, r_f = [sm[:, c:c + 1] for c in range(6)]
+        rowmax(2)
+        nc.vector.reduce_max(out=m_a, in_=m4[:, 0:3], axis=AX.X)
+        nc.vector.tensor_scalar(out=neg_a, in0=m_a, scalar1=-1.0, scalar2=None, op0=ALU.mult)
+        for k in range(3):
+            nc.scalar.activation(out=ee[:, k, :], in_=hts[k][:].rearrange("b j n -> b (j n)"), func=AF.Exp,
+                                 bias=neg_a, scale=1.0, accum_out=s4[:, k:k + 1])
+        rowmax(3)
+        nc.vector.scalar_tensor_tensor(out=neg_f, in0=m4[:, 3:4], scalar=-1.0, in1=neg_a, op0=ALU.mult, op1=ALU.min)
+        nc.scalar.activation(out=fac[:], in_=m_a, func=AF.Exp, bias=neg_f, scale=1.0)
+        nc.scalar.activation(out=ee[:, 3, :], in_=hts[3][:].rearrange("b j n -> b (j n)"), func=AF.Exp,
+                             bias=neg_f, scale=1.0, accum_out=s4[:, 3:4])
+        nc.vector.reduce_sum(out=s_a, in_=s4[:, 0:3], axis=AX.X)
+        nc.vector.scalar_tensor_tensor(out=tot, in0=s_a, scalar=fac[:, 0:1], in1=s4[:, 3:4], op0=ALU.mult, op1=ALU.add)
+        nc.vector.reciprocal(out=r_f, in_=tot)
+        nc.scalar.activation(out=ee[:, 3, :], in_=ee[:, 3, :], func=AF.Copy, scale=r_f)
+        for k in range(3):
+            nc.vector.tensor_scalar(out=ee[:, k, :], in0=ee[:, k, :], scalar1=fac[:, 0:1], scalar2=r_f,
+                                    op0=ALU.mult, op1=ALU.mult)
+            nc.sync.dma_start(out=out[:, 512 * k:512 * k + 512], in_=ee[:, k, :])
+            if k == 1:
+                nc.sync.dma_start(out=out[:, 1536:2048], in_=ee[:, 3, :])

@@ -123,12 +123,8 @@ def tile_network_w_kernel(tc, data, W1, b1, a1, W2_words, W2_scales, b2, a2,
                 nc.tensor.transpose(out=dps[:, jj, :], in_=data_sb[:, P * j:P * j + P], identity=ident_b[:])
             nc.scalar.copy(out=dataT[:, 8 * half:8 * half + 8, :], in_=dps[:])
 
-        pp3 = psum.tile([P, 8, P], BF16, name="pp3", tag="x1d")
-        for i in range(5):
-            nc.tensor.transpose(out=pp3[:, i, :], in_=p3de[:, i, :], identity=ident_b[:])
-        nc.tensor.transpose(out=pp3[:, 5, :], in_=p3raw[:, 640:768], identity=ident_b[:])
         par3 = const.tile([P, 6, 16], F32, name="par3")
-        nc.vector.tensor_copy(out=par3[:], in_=pp3[:, 0:6, 0:16])
+        der3 = const.tile([P, 4, 16], F32, name="der3")
 
         par = const.tile([P, 24, 12], F32, name="par")
         for wb in range(3):
@@ -140,8 +136,6 @@ def tile_network_w_kernel(tc, data, W1, b1, a1, W2_words, W2_scales, b2, a2,
                 in_=pp[:].bitcast(BF16)[:, :, 0:24].rearrange("p w (r e) -> p w r e", e=2))
         der = const.tile([P, 4, 4, 12], F32, name="der")
         derive(nc, [par[:, i:20:5, :] for i in range(5)], par[:, 20:24, :], [der[:, i, :, :] for i in range(4)])
-        der3 = const.tile([P, 4, 16], F32, name="der3")
-        derive(nc, [par3[:, i, :] for i in range(5)], par3[:, 5, :], [der3[:, i, :] for i in range(4)])
 
         def prm(i):
             if i < 12:
@@ -218,19 +212,26 @@ def tile_network_w_kernel(tc, data, W1, b1, a1, W2_words, W2_scales, b2, a2,
                                             scalar2=pr[t]["c4"], op0=ALU.mult, op1=ALU.add)
             st[("ll", i)] = ll
 
-        def pm(i):
+        def pm(i, tiles=(0, 1, 2, 3)):
             tt = st[("tt", i)]
             pr = prm(i)
-            for t in range(4):
+            for t in tiles:
                 nc.vector.scalar_tensor_tensor(out=tt[:, t, :], in0=tt[:, t, :], scalar=pr[t]["a0"],
                                                in1=st[("ww", i)][:, t, :], op0=ALU.mult, op1=ALU.mult)
 
-        def hq(i):
-            hb, hw, hs, g = (hb1, h1w, h1s, i) if i < 4 else (hb2, h2w, h2s, i - 4)
+        def hsum(i):
+            hb, g = (hb1, i) if i < 4 else (hb2, i - 4)
             nc.vector.tensor_tensor(out=hb[:, g, :, :], in0=st[("tt", i)][:].rearrange("q t b -> q b t"),
                                     in1=st[("ll", i)][:].rearrange("q t b -> q b t"), op=ALU.add)
+
+        def quant(i):
+            hb, hw, hs, g = (hb1, h1w, h1s, i) if i < 4 else (hb2, h2w, h2s, i - 4)
             nc.vector.quantize_mx(out=hw[:, g, :].bitcast(FP8X4), scales=hs[:, g, :],
                                   in_=hb[:, g, :, :].rearrange("q b t -> q (b t)"))
+
+        def hq(i):
+            hsum(i)
+            quant(i)
 
         acc1 = {}
 
@@ -302,6 +303,13 @@ def tile_network_w_kernel(tc, data, W1, b1, a1, W2_words, W2_scales, b2, a2,
         for c in range(4):
             mx2(c, 3)
 
+        pp3 = psum.tile([P, 8, P], BF16, name="pp3", tag="x1d")
+        for i in range(5):
+            nc.tensor.transpose(out=pp3[:, i, :], in_=p3de[:, i, :], identity=ident_b[:])
+        nc.tensor.transpose(out=pp3[:, 5, :], in_=p3raw[:, 640:768], identity=ident_b[:])
+        nc.vector.tensor_copy(out=par3[:], in_=pp3[:, 0:6, 0:16])
+        derive(nc, [par3[:, i, :] for i in range(5)], par3[:, 5, :], [der3[:, i, :] for i in range(4)])
+
         ev(4, acc2[0])
         tr(4, True)
         for i in range(4, 12):
@@ -325,14 +333,17 @@ def tile_network_w_kernel(tc, data, W1, b1, a1, W2_words, W2_scales, b2, a2,
             ab(i)
             th(i)
             if c > 0:
-                hq(i - 1)
+                hsum(i - 1)
             if c == 7:
                 lin(i, False)
                 sn(i)
             else:
                 sn(i)
                 lin(i, True)
-            pm(i)
+            pm(i, (0, 1))
+            if c > 0:
+                quant(i - 1)
+            pm(i, (2, 3))
         hq(11)
         for g in range(6, 8):
             for j in range(4):

@@ -221,8 +221,9 @@ def tile_network_w_kernel(tc, data, W1, b1, a1, W2_words, W2_scales, b2, a2,
 
         def hsum(i):
             hb, g = (hb1, i) if i < 4 else (hb2, i - 4)
-            nc.vector.tensor_tensor(out=hb[:, g, :, :], in0=st[("tt", i)][:].rearrange("q t b -> q b t"),
-                                    in1=st[("ll", i)][:].rearrange("q t b -> q b t"), op=ALU.add)
+            nc.vector.tensor_tensor(out=hb[:, g, :, :].rearrange("q (c i) t -> q c t i", i=4),
+                                    in0=st[("tt", i)][:].rearrange("q t (c i) -> q c t i", i=4),
+                                    in1=st[("ll", i)][:].rearrange("q t (c i) -> q c t i", i=4), op=ALU.add)
 
         def quant(i):
             hb, hw, hs, g = (hb1, h1w, h1s, i) if i < 4 else (hb2, h2w, h2s, i - 4)

@@ -75,12 +75,11 @@ def tile_network_w_kernel(tc, data, W1, b1, a1, W2_words, W2_scales, b2, a2,
             for jj in range(4):
                 for nb in range(2):
                     w1t[(nb, 4 * jc + jj)] = w[:, jj, 512 * nb:512 * nb + 512]
-        for g in range(2, 4):
-            for jc in range(2):
-                w = wts.tile([P, 8, 512], BF16, name="w1_q%d_%d" % (g, jc), tag="wA", align_bytes=64)
-                nc.sync.dma_start(out=w[:], in_=w1v[:, 8 * jc:8 * jc + 8, 512 * g:512 * g + 512])
-                for jj in range(8):
-                    w1t[(g, 8 * jc + jj)] = w[:, jj, :]
+        for g, j0, nj in [(2, 0, 8), (2, 8, 8), (3, 0, 8), (3, 8, 4), (3, 12, 4)]:
+            w = wts.tile([P, nj, 512], BF16, name="w1_q%d_%d" % (g, j0), tag="wA", align_bytes=64)
+            nc.sync.dma_start(out=w[:], in_=w1v[:, j0:j0 + nj, 512 * g:512 * g + 512])
+            for jj in range(nj):
+                w1t[(g, j0 + jj)] = w[:, jj, :]
 
         for q in range(4):
             nc.sync.dma_start(out=w2s[32 * q:32 * q + 16, :].bitcast(I32),

import math
from contextlib import ExitStack

import concourse.mybir as mybir
from concourse.masks import make_identity

F32 = mybir.dt.float32
BF16 = mybir.dt.bfloat16
I32 = mybir.dt.int32
U32 = mybir.dt.uint32
U8 = mybir.dt.uint8
FP8X4 = mybir.dt.float8_e4m3fn_x4
AF = mybir.ActivationFunctionType
ALU = mybir.AluOpType
AX = mybir.AxisListType

P = 128
FLOPS = 2 * 128 * (2048 * 2048 + 2048 * 4096 + 4096 * 2048)
TWO_PI = 2.0 * math.pi
INV_TWO_PI = 1.0 / TWO_PI


def derive(nc, a, bb, d):
    nc.vector.tensor_scalar(out=d[0], in0=a[1], scalar1=INV_TWO_PI, scalar2=None, op0=ALU.mult)
    nc.vector.tensor_tensor(out=d[1], in0=a[1], in1=bb, op=ALU.mult)
    nc.vector.tensor_tensor(out=d[1], in0=d[1], in1=a[2], op=ALU.add)
    nc.vector.tensor_scalar(out=d[2], in0=d[1], scalar1=INV_TWO_PI, scalar2=None, op0=ALU.mult)
    nc.vector.tensor_tensor(out=d[3], in0=a[3], in1=bb, op=ALU.mult)
    nc.vector.tensor_tensor(out=d[3], in0=d[3], in1=a[4], op=ALU.add)


def tile_network_w_kernel(tc, data, W1, b1, a1, W2_words, W2_scales, b2, a2,
                                     W3_words, W3_scales, b3, a3, out):
    nc = tc.nc
    with ExitStack() as ctx:
        const = ctx.enter_context(tc.tile_pool(name="const", bufs=1))
        wts = ctx.enter_context(tc.tile_pool(name="wts", bufs=8))
        work = ctx.enter_context(tc.tile_pool(name="work", bufs=3))
        psum = ctx.enter_context(tc.psum_pool(name="psum", bufs=1))
        ctx.enter_context(tc.manual_schedule())

        warm = const.tile([P, 1], F32, name="warm")
        nc.vector.memset(warm[:], 0.0)
        nc.scalar.activation(out=warm[:], in_=warm[:], func=AF.Silu)

        praw = const.tile([P, 3072], BF16, name="praw")
        p3raw = const.tile([P, 768], BF16, name="p3raw")
        nc.vector.memset(praw[:], 0.0)
        nc.vector.memset(p3raw[:], 0.0)
        w2s = const.tile([P, 4096], U8, name="w2s", align_bytes=64)
        w3s = const.tile([P, 2, 2048], U8, name="w3s", align_bytes=64)
        nc.vector.memset(w2s[:].bitcast(I32), 0)
        nc.vector.memset(w3s[:].rearrange("p a n -> p (a n)").bitcast(I32), 0)

        ident_b = const.tile([P, P], BF16, name="ident_b")
        make_identity(nc, ident_b[:])
        ident_f = const.tile([P, P], F32, name="ident_f")
        make_identity(nc, ident_f[:])

        data_sb = const.tile([P, 2048], BF16, name="data_sb")
        nc.sync.dma_start(out=data_sb[:], in_=data)

        nc.scalar.dma_start(out=praw[0:4, 0:2560], in_=a1.rearrange("(g r) i -> g (r i)", g=4))
        nc.scalar.dma_start(out=praw[0:4, 2560:3072], in_=b1.rearrange("(g r) -> g r", g=4))
        nc.scalar.dma_start(out=praw[4:12, 0:2560], in_=a2.rearrange("(g r) i -> g (r i)", g=8))
        nc.scalar.dma_start(out=praw[4:12, 2560:3072], in_=b2.rearrange("(g r) -> g r", g=8))
        nc.scalar.dma_start(out=p3raw[0:16, 0:640], in_=a3.rearrange("(j r) i -> j (r i)", j=16))
        nc.scalar.dma_start(out=p3raw[0:16, 640:768], in_=b3.rearrange("(j r) -> j r", j=16))

        w1v = W1.rearrange("(j p) n -> p j n", p=P)
        w1t = {}
        for jc in range(4):
            w = wts.tile([P, 4, 1024], BF16, name="w1_h_%d" % jc, tag="wA", align_bytes=64)
            nc.sync.dma_start(out=w[:], in_=w1v[:, 4 * jc:4 * jc + 4, 0:1024])
            for jj in range(4):
                for nb in range(2):
                    w1t[(nb, 4 * jc + jj)] = w[:, jj, 512 * nb:512 * nb + 512]
        for g, j0, nj in [(2, 0, 8), (2, 8, 8), (3, 0, 8), (3, 8, 4), (3, 12, 4)]:
            w = wts.tile([P, nj, 512], BF16, name="w1_q%d_%d" % (g, j0), tag="wA", align_bytes=64)
            nc.sync.dma_start(out=w[:], in_=w1v[:, j0:j0 + nj, 512 * g:512 * g + 512])
            for jj in range(nj):
                w1t[(g, j0 + jj)] = w[:, jj, :]

        for q in range(4):
            nc.sync.dma_start(out=w2s[32 * q:32 * q + 16, :].bitcast(I32),
                              in_=W2_scales[:, 4 * q:4 * q + 4, :].bitcast(I32))
        w2t = {}
        for hh in range(2):
            for g in range(4):
                w = wts.tile([P, 2048], U32, name="w2_%d_%d" % (hh, g), tag="wB", align_bytes=64)
                src = W2_words[g].rearrange("p n t -> p (n t)")[:, 8192 * hh:8192 * hh + 8192]
                nc.sync.dma_start(out=w[:].bitcast(I32), in_=src.bitcast(I32))
                w2t[(hh, g)] = w

        for a in range(2):
            for q in range(4):
                nc.sync.dma_start(out=w3s[32 * q:32 * q + 16, a, :].bitcast(I32),
                                  in_=W3_scales[4 * a:4 * a + 4, 4 * q:4 * q + 4, :].bitcast(I32))
        w3_parts = [(0, 1024, 2), (1024, 512, 4), (1536, 512, 4)]
        w3t = {}
        for n0, ncol, gper in w3_parts:
            for gc in range(8 // gper):
                w = wts.tile([P, gper, ncol], U32, name="w3_%d_%d" % (n0, gc), tag="wA", align_bytes=64)
                src = W3_words[gper * gc:gper * gc + gper].rearrange("g p n t -> p g (n t)")
                nc.sync.dma_start(out=w[:].bitcast(I32), in_=src[:, :, 4 * n0:4 * (n0 + ncol)].bitcast(I32))
                for gi in range(gper):
                    for j in range(n0 // P, (n0 + ncol) // P):
                        w3t[(j, gper * gc + gi)] = w[:, gi, P * j - n0:P * j - n0 + P]

        praw_w = praw[:].bitcast(F32)
        pde = const.tile([P, 12, P], F32, name="pde")
        nc.vector.tensor_copy(out=pde[:, 0:10, :], in_=praw_w[:, 0:1280].rearrange("r (p w) -> r w p", w=10))
        nc.vector.tensor_copy(out=pde[:, 10:12, :], in_=praw_w[:, 1280:1536].rearrange("r (p w) -> r w p", w=2))
        p3de = const.tile([P, 5, P], BF16, name="p3de")
        nc.vector.tensor_copy(out=p3de[:], in_=p3raw[:, 0:640].rearrange("r (p c) -> r c p", c=5))

        dataT = const.tile([P, 16, P], BF16, name="dataT")
        for half in range(2):
            dps = psum.tile([P, 8, P], BF16, name="dps_%d" % half, tag=("x0d", "x0a")[half])
            for jj in range(8):
                j = 8 * half + jj
                nc.tensor.transpose(out=dps[:, jj, :], in_=data_sb[:, P * j:P * j + P], identity=ident_b[:])
            nc.scalar.copy(out=dataT[:, 8 * half:8 * half + 8, :], in_=dps[:])

        par3 = const.tile([P, 6, 16], F32, name="par3")
        der3 = const.tile([P, 4, 16], F32, name="der3")

        par = const.tile([P, 24, 12], F32, name="par")
        for wb in range(3):
            pp = psum.tile([P, 4, P], F32, name="pp_%d" % wb, tag=("x1a", "x0d", "x0a")[wb])
            for wi in range(4):
                nc.tensor.transpose(out=pp[:, wi, :], in_=pde[:, 4 * wb + wi, :], identity=ident_f[:])
            nc.vector.tensor_copy(
                out=par[:, 8 * wb:8 * wb + 8, :].rearrange("p (w e) r -> p w r e", e=2),
                in_=pp[:].bitcast(BF16)[:, :, 0:24].rearrange("p w (r e) -> p w r e", e=2))
        der = const.tile([P, 4, 4, 12], F32, name="der")
        derive(nc, [par[:, i:20:5, :] for i in range(5)], par[:, 20:24, :], [der[:, i, :, :] for i in range(4)])

        def prm(i):
            if i < 12:
                return [{"b": par[:, 20 + t, i:i + 1], "a0": par[:, 5 * t, i:i + 1], "a3": par[:, 5 * t + 3, i:i + 1],
                         "a1p": der[:, 0, t, i:i + 1], "sb": der[:, 1, t, i:i + 1], "c2p": der[:, 2, t, i:i + 1],
                         "c4": der[:, 3, t, i:i + 1]} for t in range(4)]
            return [{"b": par3[:, 5, j:j + 1], "a0": par3[:, 0, j:j + 1], "a3": par3[:, 3, j:j + 1],
                     "a1p": der3[:, 0, j:j + 1], "sb": der3[:, 1, j:j + 1], "c2p": der3[:, 2, j:j + 1],
                     "c4": der3[:, 3, j:j + 1]} for j in range(4 * (i - 12), 4 * (i - 12) + 4)]

        hb1 = const.tile([P, 4, P, 4], BF16, name="hb1", align_bytes=64)
        h1w = const.tile([P, 4, P], U32, name="h1w", align_bytes=64)
        h1s = const.tile([P, 4, P], U8, name="h1s", align_bytes=64)
        hb2 = const.tile([P, 8, P, 4], BF16, name="hb2", align_bytes=64)
        h2w = const.tile([P, 8, P], U32, name="h2w", align_bytes=64)
        h2s = const.tile([P, 8, P], U8, name="h2s", align_bytes=64)

        st = {}

        def ev(i, acc):
            xs = work.tile([P, 4, P], F32, name="xs%d" % i, tag="xs")
            nc.scalar.copy(out=xs[:], in_=acc[:].rearrange("b (q t) -> b t q", t=4))
            st[("xs", i)] = xs

        def tr(i, both):
            for kind in (("d", "a") if both else ("d",)):
                xt = psum.tile([P, 4, P], F32, name="xt%s%d" % (kind, i), tag="x%d%s" % (i % 2, kind))
                for t in range(4):
                    nc.tensor.transpose(out=xt[:, t, :], in_=st[("xs", i)][:, t, :], identity=ident_f[:])
                st[("x" + kind, i)] = xt

        def cp(i):
            xc = work.tile([P, 4, P], F32, name="xc%d" % i, tag="xc")
            nc.scalar.copy(out=xc[:], in_=st[("xd", i)][:])
            st[("xd", i)] = xc
            st[("xa", i)] = xc

        def ab(i):
            kk = work.tile([P, 4, P], I32, name="kk%d" % i, tag="kk")
            ww = work.tile([P, 4, P], F32, name="ww%d" % i, tag="ww")
            x = st[("xd", i)]
            pr = prm(i)
            for t in range(4):
                nc.vector.tensor_scalar(out=kk[:, t, :], in0=x[:, t, :], scalar1=pr[t]["a1p"],
                                        scalar2=pr[t]["c2p"], op0=ALU.mult, op1=ALU.add)
            for t in range(4):
                nc.vector.scalar_tensor_tensor(out=ww[:, t, :], in0=x[:, t, :], scalar=pr[t]["a1p"],
                                               in1=kk[:, t, :], op0=ALU.mult, op1=ALU.subtract)
            st[("ww", i)] = ww

        def th(i):
            tt = work.tile([P, 4, P], F32, name="tt%d" % i, tag="tt")
            x = st[("xa", i)]
            pr = prm(i)
            for t in range(4):
                nc.scalar.activation(out=tt[:, t, :], in_=x[:, t, :], func=AF.Tanh, bias=pr[t]["b"], scale=1.0)
            st[("tt", i)] = tt

        def sn(i):
            ww = st[("ww", i)]
            pr = prm(i)
            for t in range(4):
                nc.scalar.activation(out=ww[:, t, :], in_=ww[:, t, :], func=AF.Sin, bias=pr[t]["sb"], scale=TWO_PI)

        def lin(i, on_scalar):
            ll = work.tile([P, 4, P], F32, name="ll%d" % i, tag="ll")
            pr = prm(i)
            for t in range(4):
                if on_scalar:
                    nc.scalar.activation(out=ll[:, t, :], in_=st[("xa", i)][:, t, :], func=AF.Identity,
                                         bias=pr[t]["c4"], scale=pr[t]["a3"])
                else:
                    nc.vector.tensor_scalar(out=ll[:, t, :], in0=st[("xd", i)][:, t, :], scalar1=pr[t]["a3"],
                                            scalar2=pr[t]["c4"], op0=ALU.mult, op1=ALU.add)
            st[("ll", i)] = ll

        def pm(i, tiles=(0, 1, 2, 3)):
            tt = st[("tt", i)]
            pr = prm(i)
            for t in tiles:
                nc.vector.scalar_tensor_tensor(out=tt[:, t, :], in0=tt[:, t, :], scalar=pr[t]["a0"],
                                               in1=st[("ww", i)][:, t, :], op0=ALU.mult, op1=ALU.mult)

        def hsum(i):
            hb, g = (hb1, i) if i < 4 else (hb2, i - 4)
            nc.vector.tensor_tensor(out=hb[:, g, :, :].rearrange("q (c i) t -> q c t i", i=4),
                                    in0=st[("tt", i)][:].rearrange("q t (c i) -> q c t i", i=4),
                                    in1=st[("ll", i)][:].rearrange("q t (c i) -> q c t i", i=4), op=ALU.add)

        def quant(i):
            hb, hw, hs, g = (hb1, h1w, h1s, i) if i < 4 else (hb2, h2w, h2s, i - 4)
            nc.vector.quantize_mx(out=hw[:, g, :].bitcast(FP8X4), scales=hs[:, g, :],
                                  in_=hb[:, g, :, :].rearrange("q b t -> q (b t)"))

        def hq(i):
            hsum(i)
            quant(i)

        acc1 = {}

        def l1_mm(pairs):
            for g, j in pairs:
                if j == 0:
                    acc1[g] = psum.tile([P, 512], F32, name="acc1_%d" % g, tag="a%d" % g)
                nc.tensor.matmul(out=acc1[g][:], lhsT=dataT[:, j, :], rhs=w1t[(g, j)],
                                 start=(j == 0), stop=(j == 15))

        acc2 = {}

        def mx2(c, g):
            if g == 0:
                acc2[c] = psum.tile([P, 512], F32, name="acc2_%d" % c, tag="a%d" % (c % 4))
            nc.tensor.matmul_mx(out=acc2[c][:], lhsT=h1w[:, g, :].bitcast(FP8X4), lhsT_scale=h1s[:, g, :],
                                rhs=w2t[(c // 4, g)][:, 512 * (c % 4):512 * (c % 4) + 512].bitcast(FP8X4),
                                rhs_scale=w2s[4 * g:P, 512 * c:512 * c + 512],
                                start=(g == 0), stop=(g == 3))

        x3 = {}
        x3_bank = {0: "a0", 1: "a1", 2: "a2", 3: "a3", 4: "x0d", 5: "x0a", 6: "x1d", 7: "x1a"}

        def mx3(j, g):
            if g == 0:
                if j < 8:
                    x3[j] = psum.tile([P, P], F32, name="x3_%d" % j, tag=x3_bank[j])[:]
                elif j % 4 == 0:
                    big = psum.tile([P, 4, P], F32, name="x3_%d" % j, tag=("a1" if j == 8 else "a2"))
                    for jj in range(4):
                        x3[j + jj] = big[:, jj, :]
            nc.tensor.matmul_mx(out=x3[j], lhsT=w3t[(j, g)].bitcast(FP8X4),
                                lhsT_scale=w3s[4 * (g % 4):P, g // 4, P * j:P * j + P],
                                rhs=h2w[:, g, :].bitcast(FP8X4), rhs_scale=h2s[:, g, :],
                                start=(g == 0), stop=(g == 7))

        l1_mm([(g, j) for j in range(12) for g in range(2)])
        l1_mm([(g, j) for g in range(2) for j in range(12, 16)])
        ev(0, acc1[0])
        ev(1, acc1[1])
        l1_mm([(2, j) for j in range(8)])
        tr(0, False)
        tr(1, False)
        l1_mm([(2, j) for j in range(8, 16)])
        l1_mm([(3, j) for j in range(8)])
        for i in range(3):
            cp(i)
            ab(i)
            th(i)
            lin(i, False)
            if i == 1:
                ev(2, acc1[2])
                tr(2, False)
                l1_mm([(3, j) for j in range(8, 16)])
            sn(i)
            pm(i)
            hq(i)
        ev(3, acc1[3])
        tr(3, True)
        for g in range(3):
            for c in range(4):
                mx2(c, g)
        ab(3)
        th(3)
        lin(3, False)
        sn(3)
        pm(3)
        hq(3)
        for c in range(4):
            mx2(c, 3)

        pp3 = psum.tile([P, 8, P], BF16, name="pp3", tag="x1d")
        for i in range(5):
            nc.tensor.transpose(out=pp3[:, i, :], in_=p3de[:, i, :], identity=ident_b[:])
        nc.tensor.transpose(out=pp3[:, 5, :], in_=p3raw[:, 640:768], identity=ident_b[:])
        nc.vector.tensor_copy(out=par3[:], in_=pp3[:, 0:6, 0:16])
        derive(nc, [par3[:, i, :] for i in range(5)], par3[:, 5, :], [der3[:, i, :] for i in range(4)])

        ev(4, acc2[0])
        tr(4, True)
        for i in range(4, 12):
            c = i - 4
            if c < 7:
                ev(i + 1, acc2[c + 1])
                tr(i + 1, True)
            if 4 <= c + 2 < 8:
                for g in range(4):
                    mx2(c + 2, g)
            if c == 6:
                for g in range(5):
                    for j in range(4):
                        mx3(j, g)
            if c == 7:
                for j in range(4):
                    mx3(j, 5)
                for g in range(6):
                    for j in range(4, 6):
                        mx3(j, g)
            ab(i)
            th(i)
            if c > 0:
                hsum(i - 1)
            if c == 7:
                lin(i, False)
                sn(i)
            else:
                sn(i)
                lin(i, True)
            pm(i, (0, 1))
            if c > 0:
                quant(i - 1)
            pm(i, (2, 3))
        hq(11)
        for g in range(6, 8):
            for j in range(4):
                mx3(j, g)
        for g in range(6, 8):
            for j in range(4, 6):
                mx3(j, g)
        for j in range(6, 8):
            for g in range(8):
                mx3(j, g)

        m4 = const.tile([P, 4], F32, name="m4")
        hts = {}

        def cp3(k):
            xc = work.tile([P, 4, P], F32, name="xc%d" % (12 + k), tag="xc")
            for t in range(4):
                nc.scalar.copy(out=xc[:, t, :], in_=x3[4 * k + t])
            st[("xd", 12 + k)] = xc
            st[("xa", 12 + k)] = xc

        def h3(k, by_tile):
            hh = work.tile([P, 4, P], F32, name="h3_%d" % k, tag="xs")
            ht = psum.tile([P, 4, P], F32, name="ht_%d" % k, tag=("a0", "a3", "x0d", "x0a")[k])
            tt, ll = st[("tt", 12 + k)], st[("ll", 12 + k)]
            if not by_tile:
                nc.vector.tensor_tensor(out=hh[:], in0=tt[:], in1=ll[:], op=ALU.add)
            for t in range(4):
                if by_tile:
                    nc.vector.tensor_tensor(out=hh[:, t, :], in0=tt[:, t, :], in1=ll[:, t, :], op=ALU.add)
                nc.tensor.transpose(out=ht[:, t, :], in_=hh[:, t, :], identity=ident_f[:])
            hts[k] = ht

        def rowmax(k):
            nc.vector.reduce_max(out=m4[:, k:k + 1], in_=hts[k][:].rearrange("b j n -> b (j n)"), axis=AX.X)

        cp3(0)
        for j in range(8, 16):
            for g in range(8):
                mx3(j, g)
        for k in range(4):
            i = 12 + k
            ab(i)
            th(i)
            if k >= 1:
                h3(k - 1, False)
            if k >= 2:
                rowmax(k - 2)
            sn(i)
            if k < 3:
                cp3(k + 1)
            lin(i, True)
            pm(i)
        h3(3, True)

        sm = const.tile([P, 8], F32, name="sm")
        fac = const.tile([P, 1], F32, name="fac")
        s4 = const.tile([P, 4], F32, name="s4")
        ee = const.tile([P, 4, 512], F32, name="ee")
        m_a, neg_a, neg_f, s_a, tot, r_f = [sm[:, c:c + 1] for c in range(6)]
        rowmax(2)
        nc.vector.reduce_max(out=m_a, in_=m4[:, 0:3], axis=AX.X)
        nc.vector.tensor_scalar(out=neg_a, in0=m_a, scalar1=-1.0, scalar2=None, op0=ALU.mult)
        for k in range(3):
            nc.scalar.activation(out=ee[:, k, :], in_=hts[k][:].rearrange("b j n -> b (j n)"), func=AF.Exp,
                                 bias=neg_a, scale=1.0, accum_out=s4[:, k:k + 1])
        rowmax(3)
        nc.vector.scalar_tensor_tensor(out=neg_f, in0=m4[:, 3:4], scalar=-1.0, in1=neg_a, op0=ALU.mult, op1=ALU.min)
        nc.scalar.activation(out=fac[:], in_=m_a, func=AF.Exp, bias=neg_f, scale=1.0)
        nc.scalar.activation(out=ee[:, 3, :], in_=hts[3][:].rearrange("b j n -> b (j n)"), func=AF.Exp,
                             bias=neg_f, scale=1.0, accum_out=s4[:, 3:4])
        nc.vector.reduce_sum(out=s_a, in_=s4[:, 0:3], axis=AX.X)
        nc.vector.scalar_tensor_tensor(out=tot, in0=s_a, scalar=fac[:, 0:1], in1=s4[:, 3:4], op0=ALU.mult, op1=ALU.add)
        nc.vector.reciprocal(out=r_f, in_=tot)
        nc.scalar.activation(out=ee[:, 3, :], in_=ee[:, 3, :], func=AF.Copy, scale=r_f)
        for k in range(3):
            nc.vector.tensor_scalar(out=ee[:, k, :], in0=ee[:, k, :], scalar1=fac[:, 0:1], scalar2=r_f,
                                    op0=ALU.mult, op1=ALU.mult)
            nc.sync.dma_start(out=out[:, 512 * k:512 * k + 512], in_=ee[:, k, :])
            if k == 1:
                nc.sync.dma_start(out=out[:, 1536:2048], in_=ee[:, 3, :])
